import numpy as np
import ml_dtypes


def mxq(x, axis, fmt="e4m3"):
    dtype, down = {"e4m3": (ml_dtypes.float8_e4m3fn, 7), "e5m2": (ml_dtypes.float8_e5m2, 14)}[fmt]
    v = np.moveaxis(np.asarray(x, np.float32).astype(ml_dtypes.bfloat16).astype(np.float64), axis, -1)
    blocks = v.reshape(v.shape[:-1] + (-1, 32))
    amax = np.abs(blocks).max(-1, keepdims=True)
    byte = np.maximum(np.where(amax > 0, np.frexp(amax)[1] - 1 + 127, 0) - down, 1)
    scale = np.exp2(byte - 127.0)
    codes = (blocks / scale).astype(np.float32).astype(dtype).astype(np.float64)
    return np.moveaxis((codes * scale).reshape(v.shape), -1, axis)


WIDE = False


def mx_kscale(k):
    if not WIDE:
        return np.ones(k)
    levels = np.array([30, -30])
    if k % 512:
        return np.exp2(np.random.permutation(np.resize(levels, k // 32))).repeat(32)
    a = np.empty((k // 512, 16))
    for p in range(k // 512):
        a[p, :8] = np.random.permutation(np.resize(levels, 8))
        for g in range(8):
            far = levels[np.abs(levels - a[p, g]) >= 10]
            a[p, g + 8] = far[np.random.randint(len(far))]
    return np.exp2(a.ravel()).repeat(32)


BF16 = ml_dtypes.bfloat16


def bf(x):
    return np.asarray(x, np.float32).astype(BF16)


def f64(x):
    return np.asarray(x).astype(np.float64)


E2M1 = np.array([0.0, 0.5, 1.0, 1.5, 2.0, 3.0, 4.0, 6.0, -0.0, -0.5, -1.0, -1.5, -2.0, -3.0, -4.0, -6.0])


def pack_weight(w, fmt):
    k, n = w.shape
    w = f64(bf(w)).reshape(k // 32, 32, n)
    amax = np.abs(w).max(1)
    if fmt == "e4m3":
        byte = np.frexp(amax)[1] - 1 + 127 - 7
    else:
        mant, ex = np.frexp(amax / 6.0)
        byte = np.where(mant > 0.5, ex, ex - 1) + 127
    byte = np.clip(np.where(amax > 0, byte, 1), 1, 254)
    scaled = (w * np.exp2(127.0 - byte)[:, None, :]).reshape(k, n).astype(np.float32)
    by_word = np.ascontiguousarray(scaled.reshape(k // 512, 128, 4, n).transpose(0, 1, 3, 2))
    if fmt == "e4m3":
        words = by_word.astype(ml_dtypes.float8_e4m3fn).view(np.uint8)
    else:
        c = by_word.astype(ml_dtypes.float4_e2m1fn).view(np.uint8) & 0xF
        words = c[..., 0::2] | (c[..., 1::2] << 4)
    return np.ascontiguousarray(words), np.ascontiguousarray(byte.astype(np.uint8).reshape(k // 512, 16, n))


def unpack_weight(words, scales, fmt):
    g, p, n, _ = words.shape
    if fmt == "e4m3":
        vals = np.ascontiguousarray(words).view(ml_dtypes.float8_e4m3fn).astype(np.float64)
    else:
        nib = np.empty((g, p, n, 4), np.uint8)
        nib[..., 0::2] = words & 0xF
        nib[..., 1::2] = words >> 4
        vals = E2M1[nib]
    vals = vals * np.repeat(np.exp2(scales.astype(np.float64) - 127.0), 8, axis=1)[..., None]
    return vals.transpose(0, 1, 3, 2).reshape(g * 512, n)

def pack4(w):
    words, scales = pack_weight(w, "e2m1")
    return words.reshape(words.shape[0], 128, -1), scales


def unpack4(words, scales):
    return unpack_weight(words.reshape(words.shape[0], 128, -1, 2), scales, "e2m1")


B, T, H, KV, HD = 1, 512, 16, 4, 128
D = H * HD
KVD = KV * HD
O = D + 2 * KVD
ROPE_BASE = 500000.0
CLAMP = 8.0


def rope(u):
    n = u.shape[1]
    inv = 1.0 / ROPE_BASE ** (np.arange(0, HD, 2) / HD)
    freqs = np.arange(T)[:, None] * inv[None, :]
    cos, sin = np.cos(freqs)[None, None], np.sin(freqs)[None, None]
    p = u.reshape(B, n, T, HD // 2, 2)
    a, b = p[..., 0], p[..., 1]
    return np.stack([a * cos - b * sin, a * sin + b * cos], axis=-1).reshape(B, n, T, HD)


def setup_inputs():
    s = mx_kscale(D)
    x = bf(np.random.standard_normal((B, T, D)) * s)
    w = np.random.standard_normal((O, D)) * 0.5 * CLAMP / np.sqrt(D) / s[None, :]
    words, scales = pack4(np.ascontiguousarray(w.T))
    return {"x": x, "w_qkv_words": words, "w_qkv_scales": scales}


def reference(x, w_qkv_words, w_qkv_scales):
    qkv = mxq(f64(x), 2, "e5m2") @ unpack4(w_qkv_words, w_qkv_scales)
    q = qkv[..., :D].reshape(B, T, H, HD).transpose(0, 2, 1, 3)
    k = qkv[..., D:D + KVD].reshape(B, T, KV, HD).transpose(0, 2, 1, 3)
    v = qkv[..., D + KVD:].reshape(B, T, KV, HD).transpose(0, 2, 1, 3)
    q = np.clip(rope(q), -CLAMP, CLAMP)
    k = np.clip(rope(k), -CLAMP, CLAMP)
    v = np.clip(v, -CLAMP, CLAMP)
    return q, k, v

@@ -1,0 +1,222 @@
+import math
+from contextlib import ExitStack
+
+import concourse.mybir as mybir
+from concourse.masks import make_identity
+
+T, D, HD = 512, 2048, 128
+O = 3072
+ROPE_BASE = 500000.0
+CLAMP = 8.0
+FLOPS = 2 * T * D * O
+
+F32 = mybir.dt.float32
+BF16 = mybir.dt.bfloat16
+I32 = mybir.dt.int32
+U32 = mybir.dt.uint32
+U8 = mybir.dt.uint8
+E5M2X4 = mybir.dt.float8_e5m2_x4
+E2M1X4 = mybir.dt.float4_e2m1fn_x4
+ALU = mybir.AluOpType
+ACT = mybir.ActivationFunctionType
+
+P = 128
+TILES = T // P
+PASSES = D // 512
+HALVES = 2
+N = 512
+HEADS = N // HD
+GROUPS = O // N
+V_GROUP = GROUPS - 1
+ROUND = 1.5 * 2.0**23
+
+
+def tile_dbrxattention_pa_kernel(tc, x, w_words, w_scales, q_out, k_out, v_out):
+    nc = tc.nc
+    with ExitStack() as ctx:
+        keep = ctx.enter_context(tc.tile_pool(name="keep", bufs=1))
+        work = ctx.enter_context(tc.tile_pool(name="work", bufs=4))
+        psum = ctx.enter_context(tc.psum_pool(name="psum", bufs=8))
+        ctx.enter_context(tc.manual_schedule())
+
+        signed_t = keep.tile([P, 2, TILES], F32)
+        nc.gpsimd.iota(signed_t[:, 0, :], pattern=[[-1, TILES]], base=0, channel_multiplier=-TILES,
+                       allow_small_or_imprecise_dtypes=True)
+        nc.gpsimd.iota(signed_t[:, 1, :], pattern=[[1, TILES]], base=0, channel_multiplier=TILES,
+                       allow_small_or_imprecise_dtypes=True)
+        ident = keep.tile([P, P], F32)
+        make_identity(nc, ident[:])
+
+        first_scales = keep.tile([P, PASSES, N], U8, align_bytes=64)
+        later_scales = keep.tile([P, PASSES, O - N], U8, align_bytes=64)
+        nc.vector.memset(first_scales[:].bitcast(I32), 0)
+
+        turns = keep.tile([P, TILES, 2, HD], F32)
+        whole = keep.tile([P, TILES, 2, HD], I32)
+        frac = keep.tile([P, TILES, 2, HD], F32)
+        table = keep.tile([P, TILES, 2, HD], F32)
+        ratio = ROPE_BASE ** (-2.0 / HD)
+        for i in range(4):
+            nc.vector.tensor_scalar(
+                out=turns[:, :, 0, 2 * i : 2 * i + 2], in0=signed_t[:].rearrange("p e j -> p j e"),
+                scalar1=ratio**i / (2 * math.pi), scalar2=None, op0=ALU.mult)
+        for n in (4, 16):
+            for m in (1, 2, 3):
+                nc.vector.tensor_scalar(
+                    out=turns[:, :, 0, 2 * m * n : 2 * (m + 1) * n], in0=turns[:, :, 0, 0 : 2 * n],
+                    scalar1=ratio ** (m * n), scalar2=None, op0=ALU.mult)
+
+        def reduce_turns(js):
+            nc.vector.tensor_scalar(out=turns[:, js, 1, :], in0=turns[:, js, 0, :],
+                                    scalar1=0.25, scalar2=None, op0=ALU.add)
+            nc.vector.tensor_scalar(out=whole[:, js], in0=turns[:, js], scalar1=ROUND, scalar2=ROUND,
+                                    op0=ALU.add, op1=ALU.subtract)
+            nc.vector.tensor_tensor(out=frac[:, js], in0=turns[:, js], in1=whole[:, js], op=ALU.subtract)
+
+        def sine(js):
+            nc.scalar.activation(out=table[:, js], in_=frac[:, js], func=ACT.Sin, scale=2 * math.pi)
+
+        reduce_turns(slice(0, 1))
+        sine(slice(0, 1))
+        nc.vector.memset(later_scales[:].bitcast(I32), 0)
+        reduce_turns(slice(1, TILES))
+
+        x_rows = x[0].rearrange("(p j) d -> p j d", j=TILES)
+        x_sb = {}
+        w_sb = {}
+
+        def load_x(j):
+            for h in range(HALVES):
+                half = keep.tile([P, D // HALVES], BF16, name="x_%d_%d" % (j, h))
+                nc.sync.dma_start(out=half[:], in_=x_rows[:, j, h * D // HALVES : (h + 1) * D // HALVES])
+                x_sb[j, h] = half
+
+        def load_scales(plane, first, last):
+            for r in range(4):
+                nc.sync.dma_start(
+                    out=plane[r:P:32, :, :].bitcast(I32),
+                    in_=w_scales[:, r:16:4, first:last].rearrange("g q n -> q g n").bitcast(I32))
+
+        def load_w(c):
+            words = keep.tile([P, PASSES, 2 * N], U8, name="w_%d" % c, align_bytes=64)
+            nc.sync.dma_start(
+                out=words[:].bitcast(I32),
+                in_=w_words[:, :, 2 * N * c : 2 * N * (c + 1)].rearrange("g p n -> p g n").bitcast(I32))
+            w_sb[c] = words
+
+        load_x(0)
+        load_x(1)
+        load_scales(first_scales, 0, N)
+        load_w(0)
+        load_x(2)
+        load_x(3)
+        load_scales(later_scales, N, O)
+        for c in (1, V_GROUP, 2, 3, 4):
+            load_w(c)
+
+        grouped = {}
+        codes = {}
+        scales = {}
+
+        def transpose_x(j):
+            for h in range(HALVES):
+                words = x_sb[j, h][:].bitcast(F32)
+                bank = psum.tile([P, N], F32, tag="bank")
+                for g in range(2):
+                    for u in range(2):
+                        col = (2 * g + u) * P
+                        nc.tensor.transpose(bank[:, col : col + P], words[:, 256 * g + u : 256 * (g + 1) : 2], ident[:])
+                staged = keep.tile([P, 2 * P * 4], BF16, name="grouped_%d_%d" % (j, h), align_bytes=64)
+                nc.scalar.copy(
+                    out=staged[:].bitcast(F32).rearrange("p (g r u) -> p g r u", g=2, u=2),
+                    in_=bank[:].rearrange("p (g u r) -> p g r u", g=2, u=2))
+                grouped[j, h] = staged
+
+        def quantize_x(j):
+            for h in range(HALVES):
+                code = keep.tile([P, 2 * P], U32, name="codes_%d_%d" % (j, h), align_bytes=64)
+                scale = keep.tile([P, 2 * P], U8, name="scales_%d_%d" % (j, h), align_bytes=64)
+                nc.vector.quantize_mx(out=code[:].bitcast(E5M2X4), scales=scale[:], in_=grouped[j, h][:])
+                codes[j, h] = code
+                scales[j, h] = scale
+
+        def project(c, j):
+            bank = psum.tile([P, N], F32, tag="bank")
+            for g in range(PASSES):
+                cols = slice((g % 2) * P, (g % 2 + 1) * P)
+                plane = first_scales[:, g, :] if c == 0 else later_scales[:, g, N * (c - 1) : N * c]
+                nc.tensor.matmul_mx(
+                    out=bank[:], lhsT=codes[j, g // 2][:, cols].bitcast(E5M2X4), lhsT_scale=scales[j, g // 2][:, cols],
+                    rhs=w_sb[c][:, g, :].bitcast(E2M1X4), rhs_scale=plane,
+                    start=(g == 0), stop=(g == PASSES - 1))
+            return bank
+
+        result = [keep.tile([P, HEADS, TILES, HD], F32, name="result_%d" % c) for c in range(GROUPS)]
+        targets = [q_out[0, HEADS * c : HEADS * (c + 1)] for c in range(4)] + [k_out[0], v_out[0]]
+        terms = {}
+        rotated = {}
+        v_sums = {}
+
+        def multiply(n, jj, bank):
+            if jj == 0:
+                cos_term = work.tile([P, HEADS, 2, HD], F32, tag="cos_term")
+                sin_term = work.tile([P, HEADS, 2, HD], F32, tag="sin_term")
+                terms[n] = (cos_term, sin_term)
+            cos_term, sin_term = terms[n]
+            j = 2 * (n % 2) + jj
+            pairs = bank[:].rearrange("p (h i e) -> p h i e", h=HEADS, e=2)
+            shape = [P, HEADS, HD // 2, 2]
+            sin = table[:, j, 0, :].rearrange("p (i e) -> p i e", e=2).unsqueeze(1).to_broadcast(shape)
+            cos = table[:, j, 1, :].rearrange("p (i e) -> p i e", e=2).unsqueeze(1).to_broadcast(shape)
+            nc.vector.tensor_tensor(out=cos_term[:, :, jj, :].rearrange("p h (i e) -> p h i e", e=2),
+                                    in0=pairs, in1=cos, op=ALU.mult)
+            nc.vector.tensor_tensor(out=sin_term[:, :, jj, :].rearrange("p h (i e) -> p h i e", e=2),
+                                    in0=pairs[:, :, :, ::-1], in1=sin, op=ALU.mult)
+
+        def add_terms(n, engine):
+            total = work.tile([P, HEADS, 2, HD], F32, tag="total")
+            engine.tensor_tensor(out=total[:], in0=terms[n][0][:], in1=terms[n][1][:], op=ALU.add)
+            rotated[n] = total
+
+        def clamp_and_store(c, pair, values):
+            js = slice(2 * pair, 2 * pair + 2)
+            nc.vector.tensor_scalar(out=result[c][:, :, js, :], in0=values[:], scalar1=CLAMP, scalar2=-CLAMP,
+                                    op0=ALU.min, op1=ALU.max)
+            nc.sync.dma_start(
+                out=targets[c].rearrange("h (p j) d -> p h j d", j=TILES)[:, :, js, :],
+                in_=result[c][:, :, js, :])
+
+        def project_v(j):
+            bank = project(V_GROUP, j)
+            if j % 2 == 0:
+                v_sum = work.tile([P, HEADS, 2, HD], F32, tag="v_sum", bufs=2)
+                v_sums[j // 2] = v_sum
+            nc.scalar.copy(out=v_sums[j // 2][:, :, j % 2, :], in_=bank[:].rearrange("p (h d) -> p h d", h=HEADS))
+
+        transpose_x(0)
+        transpose_x(1)
+        sine(slice(1, TILES))
+        quantize_x(0)
+        quantize_x(1)
+        multiply(0, 0, project(0, 0))
+        transpose_x(2)
+        transpose_x(3)
+        quantize_x(2)
+        quantize_x(3)
+        steps = 2 * V_GROUP
+        for n in range(steps):
+            c = n // 2
+            for jj in range(2):
+                if (n, jj) != (0, 0):
+                    multiply(n, jj, project(c, 2 * (n % 2) + jj))
+            if n % 2 == 0 and c >= 1:
+                project_v(c - 1)
+            if n < steps - 1:
+                add_terms(n, nc.gpsimd)
+            if n >= 2:
+                clamp_and_store((n - 2) // 2, n % 2, rotated[n - 2])
+            if n in (5, 9):
+                clamp_and_store(V_GROUP, n // 9, v_sums[n // 9])
+        clamp_and_store(V_GROUP - 1, 0, rotated[steps - 2])
+        add_terms(steps - 1, nc.vector)
+        clamp_and_store(V_GROUP - 1, 1, rotated[steps - 1])

@@ -28,6 +28,9 @@ N = 512
 HEADS = N // HD
 GROUPS = O // N
 V_GROUP = GROUPS - 1
+ROPE_GROUPS = GROUPS - 1
+PLANES = ((0, 1), (1, 2), (2, GROUPS))
+CLAMPS = {2: (0, (0,)), 5: (0, (1, 2, 3)), 6: (0, (4, V_GROUP)), 7: (1, (0,)), 8: (1, (1, V_GROUP)), 9: (1, (2,)), 10: (1, (3,))}
 ROUND = 1.5 * 2.0**23
 
 
@@ -47,9 +50,11 @@ def tile_dbrxattention_pa_kernel(tc, x, w_words, w_scales, q_out, k_out, v_out):
         ident = keep.tile([P, P], F32)
         make_identity(nc, ident[:])
 
-        first_scales = keep.tile([P, PASSES, N], U8, align_bytes=64)
-        later_scales = keep.tile([P, PASSES, O - N], U8, align_bytes=64)
-        nc.vector.memset(first_scales[:].bitcast(I32), 0)
+        planes = {}
+        for first, last in PLANES:
+            planes[first] = keep.tile([P, PASSES, N * (last - first)], U8, name="plane_%d" % first, align_bytes=64)
+        nc.vector.memset(planes[0][:].bitcast(I32), 0)
+        nc.vector.memset(planes[1][:].bitcast(I32), 0)
 
         turns = keep.tile([P, TILES, 2, HD], F32)
         whole = keep.tile([P, TILES, 2, HD], I32)
@@ -76,10 +81,9 @@ def tile_dbrxattention_pa_kernel(tc, x, w_words, w_scales, q_out, k_out, v_out):
         def sine(js):
             nc.scalar.activation(out=table[:, js], in_=frac[:, js], func=ACT.Sin, scale=2 * math.pi)
 
-        reduce_turns(slice(0, 1))
-        sine(slice(0, 1))
-        nc.vector.memset(later_scales[:].bitcast(I32), 0)
-        reduce_turns(slice(1, TILES))
+        reduce_turns(slice(0, 2))
+        sine(slice(0, 2))
+        nc.vector.memset(planes[2][:].bitcast(I32), 0)
 
         x_rows = x[0].rearrange("(p j) d -> p j d", j=TILES)
         x_sb = {}
@@ -91,11 +95,11 @@ def tile_dbrxattention_pa_kernel(tc, x, w_words, w_scales, q_out, k_out, v_out):
                 nc.sync.dma_start(out=half[:], in_=x_rows[:, j, h * D // HALVES : (h + 1) * D // HALVES])
                 x_sb[j, h] = half
 
-        def load_scales(plane, first, last):
+        def load_scales(first, last):
             for r in range(4):
                 nc.sync.dma_start(
-                    out=plane[r:P:32, :, :].bitcast(I32),
-                    in_=w_scales[:, r:16:4, first:last].rearrange("g q n -> q g n").bitcast(I32))
+                    out=planes[first][r:P:32, :, :].bitcast(I32),
+                    in_=w_scales[:, r:16:4, N * first : N * last].rearrange("g q n -> q g n").bitcast(I32))
 
         def load_w(c):
             words = keep.tile([P, PASSES, 2 * N], U8, name="w_%d" % c, align_bytes=64)
@@ -106,15 +110,19 @@ def tile_dbrxattention_pa_kernel(tc, x, w_words, w_scales, q_out, k_out, v_out):
 
         load_x(0)
         load_x(1)
-        load_scales(first_scales, 0, N)
+        load_scales(*PLANES[0])
         load_w(0)
+        load_scales(*PLANES[1])
+        load_w(1)
+        load_scales(*PLANES[2])
+        load_w(2)
         load_x(2)
+        load_w(3)
         load_x(3)
-        load_scales(later_scales, N, O)
-        for c in (1, V_GROUP, 2, 3, 4):
-            load_w(c)
+        load_w(4)
+        load_w(V_GROUP)
 
-        grouped = {}
+        grouped = [keep.tile([P, D], BF16, name="grouped_%d" % j, align_bytes=64) for j in range(TILES)]
         codes = {}
         scales = {}
 
@@ -126,97 +134,95 @@ def tile_dbrxattention_pa_kernel(tc, x, w_words, w_scales, q_out, k_out, v_out):
                     for u in range(2):
                         col = (2 * g + u) * P
                         nc.tensor.transpose(bank[:, col : col + P], words[:, 256 * g + u : 256 * (g + 1) : 2], ident[:])
-                staged = keep.tile([P, 2 * P * 4], BF16, name="grouped_%d_%d" % (j, h), align_bytes=64)
+                staged = grouped[j][:, h * D // HALVES : (h + 1) * D // HALVES]
                 nc.scalar.copy(
-                    out=staged[:].bitcast(F32).rearrange("p (g r u) -> p g r u", g=2, u=2),
+                    out=staged.bitcast(F32).rearrange("p (g r u) -> p g r u", g=2, u=2),
                     in_=bank[:].rearrange("p (g u r) -> p g r u", g=2, u=2))
-                grouped[j, h] = staged
 
-        def quantize_x(j):
-            for h in range(HALVES):
-                code = keep.tile([P, 2 * P], U32, name="codes_%d_%d" % (j, h), align_bytes=64)
-                scale = keep.tile([P, 2 * P], U8, name="scales_%d_%d" % (j, h), align_bytes=64)
-                nc.vector.quantize_mx(out=code[:].bitcast(E5M2X4), scales=scale[:], in_=grouped[j, h][:])
-                codes[j, h] = code
-                scales[j, h] = scale
+        def quantize_x(j, parts):
+            width = D // parts
+            for part in range(parts):
+                code = keep.tile([P, width // 4], U32, name="codes_%d_%d" % (j, part), align_bytes=64)
+                scale = keep.tile([P, width // 4], U8, name="scales_%d_%d" % (j, part), align_bytes=64)
+                nc.vector.quantize_mx(out=code[:].bitcast(E5M2X4), scales=scale[:],
+                                      in_=grouped[j][:, part * width : (part + 1) * width])
+                for g in range(PASSES // parts):
+                    codes[j, part * PASSES // parts + g] = code[:, g * P : (g + 1) * P]
+                    scales[j, part * PASSES // parts + g] = scale[:, g * P : (g + 1) * P]
 
         def project(c, j):
             bank = psum.tile([P, N], F32, tag="bank")
+            first = min(c, PLANES[-1][0])
             for g in range(PASSES):
-                cols = slice((g % 2) * P, (g % 2 + 1) * P)
-                plane = first_scales[:, g, :] if c == 0 else later_scales[:, g, N * (c - 1) : N * c]
                 nc.tensor.matmul_mx(
-                    out=bank[:], lhsT=codes[j, g // 2][:, cols].bitcast(E5M2X4), lhsT_scale=scales[j, g // 2][:, cols],
-                    rhs=w_sb[c][:, g, :].bitcast(E2M1X4), rhs_scale=plane,
+                    out=bank[:], lhsT=codes[j, g].bitcast(E5M2X4), lhsT_scale=scales[j, g],
+                    rhs=w_sb[c][:, g, :].bitcast(E2M1X4),
+                    rhs_scale=planes[first][:, g, N * (c - first) : N * (c - first + 1)],
                     start=(g == 0), stop=(g == PASSES - 1))
             return bank
 
-        result = [keep.tile([P, HEADS, TILES, HD], F32, name="result_%d" % c) for c in range(GROUPS)]
+        batches = {}
+        result = {}
+        for n, (pair, groups) in CLAMPS.items():
+            batches[n] = keep.tile([P, len(groups), HEADS, 2, HD], F32, name="batch_%d" % n)
+            for slot, c in enumerate(groups):
+                result[pair, c] = batches[n][:, slot]
         targets = [q_out[0, HEADS * c : HEADS * (c + 1)] for c in range(4)] + [k_out[0], v_out[0]]
-        terms = {}
-        rotated = {}
-        v_sums = {}
 
-        def multiply(n, jj, bank):
-            if jj == 0:
-                cos_term = work.tile([P, HEADS, 2, HD], F32, tag="cos_term")
-                sin_term = work.tile([P, HEADS, 2, HD], F32, tag="sin_term")
-                terms[n] = (cos_term, sin_term)
-            cos_term, sin_term = terms[n]
-            j = 2 * (n % 2) + jj
+        def multiply(c, j, cos_term, sin_term):
+            bank = project(c, j)
             pairs = bank[:].rearrange("p (h i e) -> p h i e", h=HEADS, e=2)
             shape = [P, HEADS, HD // 2, 2]
             sin = table[:, j, 0, :].rearrange("p (i e) -> p i e", e=2).unsqueeze(1).to_broadcast(shape)
             cos = table[:, j, 1, :].rearrange("p (i e) -> p i e", e=2).unsqueeze(1).to_broadcast(shape)
-            nc.vector.tensor_tensor(out=cos_term[:, :, jj, :].rearrange("p h (i e) -> p h i e", e=2),
+            nc.vector.tensor_tensor(out=cos_term[:, :, j % 2, :].rearrange("p h (i e) -> p h i e", e=2),
                                     in0=pairs, in1=cos, op=ALU.mult)
-            nc.vector.tensor_tensor(out=sin_term[:, :, jj, :].rearrange("p h (i e) -> p h i e", e=2),
+            nc.vector.tensor_tensor(out=sin_term[:, :, j % 2, :].rearrange("p h (i e) -> p h i e", e=2),
                                     in0=pairs[:, :, :, ::-1], in1=sin, op=ALU.mult)
 
-        def add_terms(n, engine):
-            total = work.tile([P, HEADS, 2, HD], F32, tag="total")
-            engine.tensor_tensor(out=total[:], in0=terms[n][0][:], in1=terms[n][1][:], op=ALU.add)
-            rotated[n] = total
+        def clamp(values):
+            nc.vector.tensor_scalar(out=values, in0=values, scalar1=CLAMP, scalar2=-CLAMP, op0=ALU.min, op1=ALU.max)
 
-        def clamp_and_store(c, pair, values):
-            js = slice(2 * pair, 2 * pair + 2)
-            nc.vector.tensor_scalar(out=result[c][:, :, js, :], in0=values[:], scalar1=CLAMP, scalar2=-CLAMP,
-                                    op0=ALU.min, op1=ALU.max)
-            nc.sync.dma_start(
-                out=targets[c].rearrange("h (p j) d -> p h j d", j=TILES)[:, :, js, :],
-                in_=result[c][:, :, js, :])
+        def store(pair, c, jj, values):
+            rows = targets[c].rearrange("h (p a j) d -> p a h j d", a=2, j=2)
+            nc.sync.dma_start(out=rows[:, pair, :, jj, :], in_=values)
+
+        def clamp_and_store(n):
+            pair, groups = CLAMPS[n]
+            clamp(batches[n][:].rearrange("p c h j d -> p (c h j d)"))
+            for c in groups:
+                store(pair, c, slice(0, 2), result[pair, c])
 
         def project_v(j):
             bank = project(V_GROUP, j)
-            if j % 2 == 0:
-                v_sum = work.tile([P, HEADS, 2, HD], F32, tag="v_sum", bufs=2)
-                v_sums[j // 2] = v_sum
-            nc.scalar.copy(out=v_sums[j // 2][:, :, j % 2, :], in_=bank[:].rearrange("p (h d) -> p h d", h=HEADS))
+            nc.scalar.copy(out=result[j // 2, V_GROUP][:, :, j % 2, :], in_=bank[:].rearrange("p (h d) -> p h d", h=HEADS))
 
         transpose_x(0)
         transpose_x(1)
-        sine(slice(1, TILES))
-        quantize_x(0)
-        quantize_x(1)
-        multiply(0, 0, project(0, 0))
-        transpose_x(2)
-        transpose_x(3)
-        quantize_x(2)
-        quantize_x(3)
-        steps = 2 * V_GROUP
-        for n in range(steps):
-            c = n // 2
+        quantize_x(0, HALVES)
+        quantize_x(1, HALVES)
+        reduce_turns(slice(2, TILES))
+        sine(slice(2, TILES))
+        last = 2 * ROPE_GROUPS - 1
+        for n in range(last + 1):
+            pair, c = divmod(n, ROPE_GROUPS)
+            cos_term = work.tile([P, HEADS, 2, HD], F32, tag="cos_term")
+            sin_term = work.tile([P, HEADS, 2, HD], F32, tag="sin_term")
             for jj in range(2):
-                if (n, jj) != (0, 0):
-                    multiply(n, jj, project(c, 2 * (n % 2) + jj))
-            if n % 2 == 0 and c >= 1:
-                project_v(c - 1)
-            if n < steps - 1:
-                add_terms(n, nc.gpsimd)
-            if n >= 2:
-                clamp_and_store((n - 2) // 2, n % 2, rotated[n - 2])
-            if n in (5, 9):
-                clamp_and_store(V_GROUP, n // 9, v_sums[n // 9])
-        clamp_and_store(V_GROUP - 1, 0, rotated[steps - 2])
-        add_terms(steps - 1, nc.vector)
-        clamp_and_store(V_GROUP - 1, 1, rotated[steps - 1])
+                multiply(c, 2 * pair + jj, cos_term, sin_term)
+            if n in (3, 4):
+                quantize_x(n - 1, 1)
+            if n in CLAMPS:
+                clamp_and_store(n)
+            if n < last:
+                nc.gpsimd.tensor_tensor(out=result[pair, c], in0=cos_term[:], in1=sin_term[:], op=ALU.add)
+            if n in (2, 3):
+                transpose_x(n)
+            if 4 <= n < 8:
+                project_v(n - 4)
+        clamp_and_store(last + 1)
+        for jj in range(2):
+            values = keep.tile([P, HEADS, HD], F32, name="last_%d" % jj)
+            nc.vector.tensor_tensor(out=values[:], in0=cos_term[:, :, jj, :], in1=sin_term[:, :, jj, :], op=ALU.add)
+            clamp(values[:])
+            store(1, c, jj, values[:])

@@ -30,7 +30,9 @@ GROUPS = O // N
 V_GROUP = GROUPS - 1
 ROPE_GROUPS = GROUPS - 1
 PLANES = ((0, 1), (1, 2), (2, GROUPS))
-CLAMPS = {2: (0, (0,)), 5: (0, (1, 2, 3)), 6: (0, (4, V_GROUP)), 7: (1, (0,)), 8: (1, (1, V_GROUP)), 9: (1, (2,)), 10: (1, (3,))}
+STEPS = 2 * ROPE_GROUPS
+LAG = 2
+V_PARTNER = 2
 ROUND = 1.5 * 2.0**23
 
 
@@ -54,7 +56,6 @@ def tile_dbrxattention_pa_kernel(tc, x, w_words, w_scales, q_out, k_out, v_out):
         for first, last in PLANES:
             planes[first] = keep.tile([P, PASSES, N * (last - first)], U8, name="plane_%d" % first, align_bytes=64)
         nc.vector.memset(planes[0][:].bitcast(I32), 0)
-        nc.vector.memset(planes[1][:].bitcast(I32), 0)
 
         turns = keep.tile([P, TILES, 2, HD], F32)
         whole = keep.tile([P, TILES, 2, HD], I32)
@@ -83,6 +84,7 @@ def tile_dbrxattention_pa_kernel(tc, x, w_words, w_scales, q_out, k_out, v_out):
 
         reduce_turns(slice(0, 2))
         sine(slice(0, 2))
+        nc.vector.memset(planes[1][:].bitcast(I32), 0)
         nc.vector.memset(planes[2][:].bitcast(I32), 0)
 
         x_rows = x[0].rearrange("(p j) d -> p j d", j=TILES)
@@ -112,15 +114,13 @@ def tile_dbrxattention_pa_kernel(tc, x, w_words, w_scales, q_out, k_out, v_out):
         load_x(1)
         load_scales(*PLANES[0])
         load_w(0)
+        load_x(2)
+        load_x(3)
         load_scales(*PLANES[1])
         load_w(1)
         load_scales(*PLANES[2])
-        load_w(2)
-        load_x(2)
-        load_w(3)
-        load_x(3)
-        load_w(4)
-        load_w(V_GROUP)
+        for c in (V_GROUP, 2, 3, 4):
+            load_w(c)
 
         grouped = [keep.tile([P, D], BF16, name="grouped_%d" % j, align_bytes=64) for j in range(TILES)]
         codes = {}
@@ -163,10 +163,13 @@ def tile_dbrxattention_pa_kernel(tc, x, w_words, w_scales, q_out, k_out, v_out):
 
         batches = {}
         result = {}
-        for n, (pair, groups) in CLAMPS.items():
-            batches[n] = keep.tile([P, len(groups), HEADS, 2, HD], F32, name="batch_%d" % n)
-            for slot, c in enumerate(groups):
-                result[pair, c] = batches[n][:, slot]
+        for n in range(STEPS - 1):
+            c, pair = divmod(n, 2)
+            groups = (c, V_GROUP) if c == V_PARTNER else (c,)
+            batch = keep.tile([P, len(groups), HEADS, 2, HD], F32, name="batch_%d" % n)
+            batches[n] = (batch, groups)
+            for slot, group in enumerate(groups):
+                result[pair, group] = batch[:, slot]
         targets = [q_out[0, HEADS * c : HEADS * (c + 1)] for c in range(4)] + [k_out[0], v_out[0]]
 
         def multiply(c, j, cos_term, sin_term):
@@ -188,10 +191,10 @@ def tile_dbrxattention_pa_kernel(tc, x, w_words, w_scales, q_out, k_out, v_out):
             nc.sync.dma_start(out=rows[:, pair, :, jj, :], in_=values)
 
         def clamp_and_store(n):
-            pair, groups = CLAMPS[n]
-            clamp(batches[n][:].rearrange("p c h j d -> p (c h j d)"))
+            batch, groups = batches[n]
+            clamp(batch[:].rearrange("p c h j d -> p (c h j d)"))
             for c in groups:
-                store(pair, c, slice(0, 2), result[pair, c])
+                store(n % 2, c, slice(0, 2), result[n % 2, c])
 
         def project_v(j):
             bank = project(V_GROUP, j)
@@ -201,26 +204,26 @@ def tile_dbrxattention_pa_kernel(tc, x, w_words, w_scales, q_out, k_out, v_out):
         transpose_x(1)
         quantize_x(0, HALVES)
         quantize_x(1, HALVES)
-        reduce_turns(slice(2, TILES))
-        sine(slice(2, TILES))
-        last = 2 * ROPE_GROUPS - 1
-        for n in range(last + 1):
-            pair, c = divmod(n, ROPE_GROUPS)
+        for n in range(STEPS):
+            c, pair = divmod(n, 2)
             cos_term = work.tile([P, HEADS, 2, HD], F32, tag="cos_term")
             sin_term = work.tile([P, HEADS, 2, HD], F32, tag="sin_term")
-            for jj in range(2):
-                multiply(c, 2 * pair + jj, cos_term, sin_term)
-            if n in (3, 4):
-                quantize_x(n - 1, 1)
-            if n in CLAMPS:
-                clamp_and_store(n)
-            if n < last:
+            multiply(c, 2 * pair, cos_term, sin_term)
+            if n == 0:
+                reduce_turns(slice(2, TILES))
+                transpose_x(2)
+                transpose_x(3)
+                sine(slice(2, TILES))
+                quantize_x(2, HALVES)
+                quantize_x(3, HALVES)
+            multiply(c, 2 * pair + 1, cos_term, sin_term)
+            if n >= LAG:
+                clamp_and_store(n - LAG)
+            if n < STEPS - 1:
                 nc.gpsimd.tensor_tensor(out=result[pair, c], in0=cos_term[:], in1=sin_term[:], op=ALU.add)
-            if n in (2, 3):
-                transpose_x(n)
-            if 4 <= n < 8:
-                project_v(n - 4)
-        clamp_and_store(last + 1)
+            if 2 <= n < 2 + TILES:
+                project_v(n - 2)
+        clamp_and_store(STEPS - 2)
         for jj in range(2):
             values = keep.tile([P, HEADS, HD], F32, name="last_%d" % jj)
             nc.vector.tensor_tensor(out=values[:], in0=cos_term[:, :, jj, :], in1=sin_term[:, :, jj, :], op=ALU.add)

@@ -33,6 +33,8 @@ PLANES = ((0, 1), (1, 2), (2, GROUPS))
 STEPS = 2 * ROPE_GROUPS
 LAG = 2
 V_PARTNER = 2
+WARM_N = 256
+PAIRS = HD // 2
 ROUND = 1.5 * 2.0**23
 
 
@@ -44,46 +46,51 @@ def tile_dbrxattention_pa_kernel(tc, x, w_words, w_scales, q_out, k_out, v_out):
         psum = ctx.enter_context(tc.psum_pool(name="psum", bufs=8))
         ctx.enter_context(tc.manual_schedule())
 
-        signed_t = keep.tile([P, 2, TILES], F32)
-        nc.gpsimd.iota(signed_t[:, 0, :], pattern=[[-1, TILES]], base=0, channel_multiplier=-TILES,
-                       allow_small_or_imprecise_dtypes=True)
-        nc.gpsimd.iota(signed_t[:, 1, :], pattern=[[1, TILES]], base=0, channel_multiplier=TILES,
+        position = keep.tile([P, TILES], F32)
+        nc.gpsimd.iota(position[:], pattern=[[1, TILES]], base=0, channel_multiplier=TILES,
                        allow_small_or_imprecise_dtypes=True)
         ident = keep.tile([P, P], F32)
         make_identity(nc, ident[:])
+
+        zeros = keep.tile([P, WARM_N], F32)
+        nc.vector.memset(zeros[:], 0.0)
+        unread = psum.tile([P, N], F32, tag="bank")
+
+        def warm_up():
+            nc.tensor.matmul(unread[:, 0:WARM_N], lhsT=zeros[:, 0:P], rhs=zeros[:], start=True, stop=True)
 
         planes = {}
         for first, last in PLANES:
             planes[first] = keep.tile([P, PASSES, N * (last - first)], U8, name="plane_%d" % first, align_bytes=64)
         nc.vector.memset(planes[0][:].bitcast(I32), 0)
 
-        turns = keep.tile([P, TILES, 2, HD], F32)
-        whole = keep.tile([P, TILES, 2, HD], I32)
-        frac = keep.tile([P, TILES, 2, HD], F32)
-        table = keep.tile([P, TILES, 2, HD], F32)
+        turns = keep.tile([P, 2, TILES, PAIRS], F32)
+        whole = keep.tile([P, 2, TILES, PAIRS], I32)
+        frac = keep.tile([P, 2, TILES, PAIRS], F32)
+        cos_table = keep.tile([P, TILES, PAIRS, 2], F32)
+        sin_table = keep.tile([P, TILES, PAIRS, 2], F32)
         ratio = ROPE_BASE ** (-2.0 / HD)
         for i in range(4):
             nc.vector.tensor_scalar(
-                out=turns[:, :, 0, 2 * i : 2 * i + 2], in0=signed_t[:].rearrange("p e j -> p j e"),
+                out=turns[:, 0, :, i : i + 1], in0=position[:].unsqueeze(2),
                 scalar1=ratio**i / (2 * math.pi), scalar2=None, op0=ALU.mult)
         for n in (4, 16):
             for m in (1, 2, 3):
                 nc.vector.tensor_scalar(
-                    out=turns[:, :, 0, 2 * m * n : 2 * (m + 1) * n], in0=turns[:, :, 0, 0 : 2 * n],
+                    out=turns[:, 0, :, m * n : (m + 1) * n], in0=turns[:, 0, :, 0:n],
                     scalar1=ratio ** (m * n), scalar2=None, op0=ALU.mult)
+        nc.vector.tensor_scalar(out=turns[:, 1], in0=turns[:, 0], scalar1=0.25, scalar2=None, op0=ALU.add)
+        nc.vector.tensor_scalar(out=whole[:], in0=turns[:], scalar1=ROUND, scalar2=ROUND, op0=ALU.add, op1=ALU.subtract)
+        nc.vector.tensor_tensor(out=frac[:], in0=turns[:], in1=whole[:], op=ALU.subtract)
 
-        def reduce_turns(js):
-            nc.vector.tensor_scalar(out=turns[:, js, 1, :], in0=turns[:, js, 0, :],
-                                    scalar1=0.25, scalar2=None, op0=ALU.add)
-            nc.vector.tensor_scalar(out=whole[:, js], in0=turns[:, js], scalar1=ROUND, scalar2=ROUND,
-                                    op0=ALU.add, op1=ALU.subtract)
-            nc.vector.tensor_tensor(out=frac[:, js], in0=turns[:, js], in1=whole[:, js], op=ALU.subtract)
+        def fill_tables(js):
+            both = frac[:, 1, js, :].unsqueeze(3).to_broadcast([P, 2, PAIRS, 2])
+            nc.scalar.activation(out=cos_table[:, js], in_=both, func=ACT.Sin, scale=2 * math.pi)
+            for e, sign in enumerate((-1, 1)):
+                nc.scalar.activation(out=sin_table[:, js, :, e], in_=frac[:, 0, js, :], func=ACT.Sin,
+                                     scale=sign * 2 * math.pi)
 
-        def sine(js):
-            nc.scalar.activation(out=table[:, js], in_=frac[:, js], func=ACT.Sin, scale=2 * math.pi)
-
-        reduce_turns(slice(0, 2))
-        sine(slice(0, 2))
+        fill_tables(slice(0, 2))
         nc.vector.memset(planes[1][:].bitcast(I32), 0)
         nc.vector.memset(planes[2][:].bitcast(I32), 0)
 
@@ -176,8 +183,8 @@ def tile_dbrxattention_pa_kernel(tc, x, w_words, w_scales, q_out, k_out, v_out):
             bank = project(c, j)
             pairs = bank[:].rearrange("p (h i e) -> p h i e", h=HEADS, e=2)
             shape = [P, HEADS, HD // 2, 2]
-            sin = table[:, j, 0, :].rearrange("p (i e) -> p i e", e=2).unsqueeze(1).to_broadcast(shape)
-            cos = table[:, j, 1, :].rearrange("p (i e) -> p i e", e=2).unsqueeze(1).to_broadcast(shape)
+            sin = sin_table[:, j].unsqueeze(1).to_broadcast(shape)
+            cos = cos_table[:, j].unsqueeze(1).to_broadcast(shape)
             nc.vector.tensor_tensor(out=cos_term[:, :, j % 2, :].rearrange("p h (i e) -> p h i e", e=2),
                                     in0=pairs, in1=cos, op=ALU.mult)
             nc.vector.tensor_tensor(out=sin_term[:, :, j % 2, :].rearrange("p h (i e) -> p h i e", e=2),
@@ -200,8 +207,12 @@ def tile_dbrxattention_pa_kernel(tc, x, w_words, w_scales, q_out, k_out, v_out):
             bank = project(V_GROUP, j)
             nc.scalar.copy(out=result[j // 2, V_GROUP][:, :, j % 2, :], in_=bank[:].rearrange("p (h d) -> p h d", h=HEADS))
 
+        warm_up()
+        warm_up()
         transpose_x(0)
+        warm_up()
         transpose_x(1)
+        warm_up()
         quantize_x(0, HALVES)
         quantize_x(1, HALVES)
         for n in range(STEPS):
@@ -210,10 +221,9 @@ def tile_dbrxattention_pa_kernel(tc, x, w_words, w_scales, q_out, k_out, v_out):
             sin_term = work.tile([P, HEADS, 2, HD], F32, tag="sin_term")
             multiply(c, 2 * pair, cos_term, sin_term)
             if n == 0:
-                reduce_turns(slice(2, TILES))
                 transpose_x(2)
                 transpose_x(3)
-                sine(slice(2, TILES))
+                fill_tables(slice(2, TILES))
                 quantize_x(2, HALVES)
                 quantize_x(3, HALVES)
             multiply(c, 2 * pair + 1, cos_term, sin_term)

import math
from contextlib import ExitStack

import concourse.mybir as mybir
from concourse.masks import make_identity

T, D, HD = 512, 2048, 128
O = 3072
ROPE_BASE = 500000.0
CLAMP = 8.0
FLOPS = 2 * T * D * O

F32 = mybir.dt.float32
BF16 = mybir.dt.bfloat16
I32 = mybir.dt.int32
U32 = mybir.dt.uint32
U8 = mybir.dt.uint8
E5M2X4 = mybir.dt.float8_e5m2_x4
E2M1X4 = mybir.dt.float4_e2m1fn_x4
ALU = mybir.AluOpType
ACT = mybir.ActivationFunctionType

P = 128
TILES = T // P
PASSES = D // 512
HALVES = 2
N = 512
HEADS = N // HD
GROUPS = O // N
V_GROUP = GROUPS - 1
ROPE_GROUPS = GROUPS - 1
PLANES = ((0, 1), (1, 2), (2, GROUPS))
STEPS = 2 * ROPE_GROUPS
LAG = 2
V_PARTNER = 2
WARM_N = 256
PAIRS = HD // 2
ROUND = 1.5 * 2.0**23


def tile_dbrxattention_pa_kernel(tc, x, w_words, w_scales, q_out, k_out, v_out):
    nc = tc.nc
    with ExitStack() as ctx:
        keep = ctx.enter_context(tc.tile_pool(name="keep", bufs=1))
        work = ctx.enter_context(tc.tile_pool(name="work", bufs=4))
        psum = ctx.enter_context(tc.psum_pool(name="psum", bufs=8))
        ctx.enter_context(tc.manual_schedule())

        position = keep.tile([P, TILES], F32)
        nc.gpsimd.iota(position[:], pattern=[[1, TILES]], base=0, channel_multiplier=TILES,
                       allow_small_or_imprecise_dtypes=True)
        ident = keep.tile([P, P], F32)
        make_identity(nc, ident[:])

        zeros = keep.tile([P, WARM_N], F32)
        nc.vector.memset(zeros[:], 0.0)
        unread = psum.tile([P, N], F32, tag="bank")

        def warm_up():
            nc.tensor.matmul(unread[:, 0:WARM_N], lhsT=zeros[:, 0:P], rhs=zeros[:], start=True, stop=True)

        planes = {}
        for first, last in PLANES:
            planes[first] = keep.tile([P, PASSES, N * (last - first)], U8, name="plane_%d" % first, align_bytes=64)
        nc.vector.memset(planes[0][:].bitcast(I32), 0)

        turns = keep.tile([P, 2, TILES, PAIRS], F32)
        whole = keep.tile([P, 2, TILES, PAIRS], I32)
        frac = keep.tile([P, 2, TILES, PAIRS], F32)
        cos_table = keep.tile([P, TILES, PAIRS, 2], F32)
        sin_table = keep.tile([P, TILES, PAIRS, 2], F32)
        ratio = ROPE_BASE ** (-2.0 / HD)
        for i in range(4):
            nc.vector.tensor_scalar(
                out=turns[:, 0, :, i : i + 1], in0=position[:].unsqueeze(2),
                scalar1=ratio**i / (2 * math.pi), scalar2=None, op0=ALU.mult)
        for n in (4, 16):
            for m in (1, 2, 3):
                nc.vector.tensor_scalar(
                    out=turns[:, 0, :, m * n : (m + 1) * n], in0=turns[:, 0, :, 0:n],
                    scalar1=ratio ** (m * n), scalar2=None, op0=ALU.mult)
        nc.vector.tensor_scalar(out=turns[:, 1], in0=turns[:, 0], scalar1=0.25, scalar2=None, op0=ALU.add)
        nc.vector.tensor_scalar(out=whole[:], in0=turns[:], scalar1=ROUND, scalar2=ROUND, op0=ALU.add, op1=ALU.subtract)
        nc.vector.tensor_tensor(out=frac[:], in0=turns[:], in1=whole[:], op=ALU.subtract)

        def fill_tables(js):
            both = frac[:, 1, js, :].unsqueeze(3).to_broadcast([P, 2, PAIRS, 2])
            nc.scalar.activation(out=cos_table[:, js], in_=both, func=ACT.Sin, scale=2 * math.pi)
            for e, sign in enumerate((-1, 1)):
                nc.scalar.activation(out=sin_table[:, js, :, e], in_=frac[:, 0, js, :], func=ACT.Sin,
                                     scale=sign * 2 * math.pi)

        fill_tables(slice(0, 2))
        nc.vector.memset(planes[1][:].bitcast(I32), 0)
        nc.vector.memset(planes[2][:].bitcast(I32), 0)

        x_rows = x[0].rearrange("(p j) d -> p j d", j=TILES)
        x_sb = {}
        w_sb = {}

        def load_x(j):
            for h in range(HALVES):
                half = keep.tile([P, D // HALVES], BF16, name="x_%d_%d" % (j, h))
                nc.sync.dma_start(out=half[:], in_=x_rows[:, j, h * D // HALVES : (h + 1) * D // HALVES])
                x_sb[j, h] = half

        def load_scales(first, last):
            for r in range(4):
                nc.sync.dma_start(
                    out=planes[first][r:P:32, :, :].bitcast(I32),
                    in_=w_scales[:, r:16:4, N * first : N * last].rearrange("g q n -> q g n").bitcast(I32))

        def load_w(c):
            words = keep.tile([P, PASSES, 2 * N], U8, name="w_%d" % c, align_bytes=64)
            nc.sync.dma_start(
                out=words[:].bitcast(I32),
                in_=w_words[:, :, 2 * N * c : 2 * N * (c + 1)].rearrange("g p n -> p g n").bitcast(I32))
            w_sb[c] = words

        load_x(0)
        load_x(1)
        load_scales(*PLANES[0])
        load_w(0)
        load_x(2)
        load_x(3)
        load_scales(*PLANES[1])
        load_w(1)
        load_scales(*PLANES[2])
        for c in (V_GROUP, 2, 3, 4):
            load_w(c)

        grouped = [keep.tile([P, D], BF16, name="grouped_%d" % j, align_bytes=64) for j in range(TILES)]
        codes = {}
        scales = {}

        def transpose_x(j):
            for h in range(HALVES):
                words = x_sb[j, h][:].bitcast(F32)
                bank = psum.tile([P, N], F32, tag="bank")
                for g in range(2):
                    for u in range(2):
                        col = (2 * g + u) * P
                        nc.tensor.transpose(bank[:, col : col + P], words[:, 256 * g + u : 256 * (g + 1) : 2], ident[:])
                staged = grouped[j][:, h * D // HALVES : (h + 1) * D // HALVES]
                nc.scalar.copy(
                    out=staged.bitcast(F32).rearrange("p (g r u) -> p g r u", g=2, u=2),
                    in_=bank[:].rearrange("p (g u r) -> p g r u", g=2, u=2))

        def quantize_x(j, parts):
            width = D // parts
            for part in range(parts):
                code = keep.tile([P, width // 4], U32, name="codes_%d_%d" % (j, part), align_bytes=64)
                scale = keep.tile([P, width // 4], U8, name="scales_%d_%d" % (j, part), align_bytes=64)
                nc.vector.quantize_mx(out=code[:].bitcast(E5M2X4), scales=scale[:],
                                      in_=grouped[j][:, part * width : (part + 1) * width])
                for g in range(PASSES // parts):
                    codes[j, part * PASSES // parts + g] = code[:, g * P : (g + 1) * P]
                    scales[j, part * PASSES // parts + g] = scale[:, g * P : (g + 1) * P]

        def project(c, j):
            bank = psum.tile([P, N], F32, tag="bank")
            first = min(c, PLANES[-1][0])
            for g in range(PASSES):
                nc.tensor.matmul_mx(
                    out=bank[:], lhsT=codes[j, g].bitcast(E5M2X4), lhsT_scale=scales[j, g],
                    rhs=w_sb[c][:, g, :].bitcast(E2M1X4),
                    rhs_scale=planes[first][:, g, N * (c - first) : N * (c - first + 1)],
                    start=(g == 0), stop=(g == PASSES - 1))
            return bank

        batches = {}
        result = {}
        for n in range(STEPS - 1):
            c, pair = divmod(n, 2)
            groups = (c, V_GROUP) if c == V_PARTNER else (c,)
            batch = keep.tile([P, len(groups), HEADS, 2, HD], F32, name="batch_%d" % n)
            batches[n] = (batch, groups)
            for slot, group in enumerate(groups):
                result[pair, group] = batch[:, slot]
        targets = [q_out[0, HEADS * c : HEADS * (c + 1)] for c in range(4)] + [k_out[0], v_out[0]]

        def multiply(c, j, cos_term, sin_term):
            bank = project(c, j)
            pairs = bank[:].rearrange("p (h i e) -> p h i e", h=HEADS, e=2)
            shape = [P, HEADS, HD // 2, 2]
            sin = sin_table[:, j].unsqueeze(1).to_broadcast(shape)
            cos = cos_table[:, j].unsqueeze(1).to_broadcast(shape)
            nc.vector.tensor_tensor(out=cos_term[:, :, j % 2, :].rearrange("p h (i e) -> p h i e", e=2),
                                    in0=pairs, in1=cos, op=ALU.mult)
            nc.vector.tensor_tensor(out=sin_term[:, :, j % 2, :].rearrange("p h (i e) -> p h i e", e=2),
                                    in0=pairs[:, :, :, ::-1], in1=sin, op=ALU.mult)

        def clamp(values):
            nc.vector.tensor_scalar(out=values, in0=values, scalar1=CLAMP, scalar2=-CLAMP, op0=ALU.min, op1=ALU.max)

        def store(pair, c, jj, values):
            rows = targets[c].rearrange("h (p a j) d -> p a h j d", a=2, j=2)
            nc.sync.dma_start(out=rows[:, pair, :, jj, :], in_=values)

        def clamp_and_store(n):
            batch, groups = batches[n]
            clamp(batch[:].rearrange("p c h j d -> p (c h j d)"))
            for c in groups:
                store(n % 2, c, slice(0, 2), result[n % 2, c])

        def project_v(j):
            bank = project(V_GROUP, j)
            nc.scalar.copy(out=result[j // 2, V_GROUP][:, :, j % 2, :], in_=bank[:].rearrange("p (h d) -> p h d", h=HEADS))

        warm_up()
        warm_up()
        transpose_x(0)
        warm_up()
        transpose_x(1)
        warm_up()
        quantize_x(0, HALVES)
        quantize_x(1, HALVES)
        for n in range(STEPS):
            c, pair = divmod(n, 2)
            cos_term = work.tile([P, HEADS, 2, HD], F32, tag="cos_term")
            sin_term = work.tile([P, HEADS, 2, HD], F32, tag="sin_term")
            multiply(c, 2 * pair, cos_term, sin_term)
            if n == 0:
                transpose_x(2)
                transpose_x(3)
                fill_tables(slice(2, TILES))
                quantize_x(2, HALVES)
                quantize_x(3, HALVES)
            multiply(c, 2 * pair + 1, cos_term, sin_term)
            if n >= LAG:
                clamp_and_store(n - LAG)
            if n < STEPS - 1:
                nc.gpsimd.tensor_tensor(out=result[pair, c], in0=cos_term[:], in1=sin_term[:], op=ALU.add)
            if 2 <= n < 2 + TILES:
                project_v(n - 2)
        clamp_and_store(STEPS - 2)
        for jj in range(2):
            values = keep.tile([P, HEADS, HD], F32, name="last_%d" % jj)
            nc.vector.tensor_tensor(out=values[:], in0=cos_term[:, :, jj, :], in1=sin_term[:, :, jj, :], op=ALU.add)
            clamp(values[:])
            store(1, c, jj, values[:])
